import numpy as np
import ml_dtypes


def mxq(x, axis, fmt="e4m3"):
    dtype, down = {"e4m3": (ml_dtypes.float8_e4m3fn, 7), "e5m2": (ml_dtypes.float8_e5m2, 14)}[fmt]
    v = np.moveaxis(np.asarray(x, np.float32).astype(ml_dtypes.bfloat16).astype(np.float64), axis, -1)
    blocks = v.reshape(v.shape[:-1] + (-1, 32))
    amax = np.abs(blocks).max(-1, keepdims=True)
    byte = np.maximum(np.where(amax > 0, np.frexp(amax)[1] - 1 + 127, 0) - down, 1)
    scale = np.exp2(byte - 127.0)
    codes = (blocks / scale).astype(np.float32).astype(dtype).astype(np.float64)
    return np.moveaxis((codes * scale).reshape(v.shape), -1, axis)


WIDE = False


def mx_kscale(k):
    if not WIDE:
        return np.ones(k)
    levels = np.array([10, -10, 5, -5, 0])
    a = np.random.permutation(np.resize(levels, k // 512 * 4)).reshape(k // 512, 4)
    idx = np.arange(k)
    return np.exp2(a[idx // 512, idx % 128 // 32])


BF16 = ml_dtypes.bfloat16


def bf(x):
    return np.asarray(x, np.float32).astype(BF16)


def f64(x):
    return np.asarray(x).astype(np.float64)


B, A, E, P, R = 128, 8, 8192, 512, 256


def setup_inputs():
    s_src, s_edge = mx_kscale(E), mx_kscale(E)
    t = mx_kscale(P)
    s_cat = np.concatenate([s_src, s_edge])
    return {
        "image_features": bf(np.random.standard_normal((B, E)) * s_src),
        "edge_attributes": bf(np.random.standard_normal((B, A, E)) * s_edge),
        "linear_w": bf(np.random.standard_normal((P, 2 * E)) / np.sqrt(2 * E) / s_cat * t[:, None]),
        "linear_b": bf(np.random.standard_normal(P) * 0.3 * t),
        "fwd_proj": bf(np.random.standard_normal((A, P, R)) / np.sqrt(P) / t[:, None]),
    }


def reference(image_features, edge_attributes, linear_w, linear_b, fwd_proj):
    w = f64(linear_w)
    node = mxq(f64(image_features), 1, "e4m3") @ mxq(w[:, :E].T, 0, "e4m3")
    edge = (mxq(f64(edge_attributes).reshape(B * A, E), 1, "e4m3") @ mxq(w[:, E:].T, 0, "e4m3")).reshape(B, A, P)
    agg = node[:, None, :] + edge + f64(linear_b)
    rep = mxq(agg.transpose(1, 0, 2), 2, "e4m3") @ mxq(f64(fwd_proj), 1, "e4m3")
    return rep.transpose(1, 0, 2)

@@ -1,0 +1,323 @@
+from contextlib import ExitStack
+
+import concourse.mybir as mybir
+from concourse.masks import make_identity
+
+F32 = mybir.dt.float32
+BF16 = mybir.dt.bfloat16
+U32 = mybir.dt.uint32
+U8 = mybir.dt.uint8
+FP8X4 = mybir.dt.float8_e4m3fn_x4
+
+NODES = 128
+TYPES = 8
+FEATURES = 8192
+HIDDEN = 512
+REP = 256
+
+P = 128
+PACK = 4
+K_PASS = P * PACK
+PASSES = FEATURES // K_PASS
+PASS_WORDS = K_PASS // 2
+BANK = 512
+
+CHUNK_PASSES = 4
+CHUNK = CHUNK_PASSES * K_PASS
+CHUNKS = FEATURES // CHUNK
+CHUNK_WORDS = CHUNK // 2
+RAW_BUFS = 6
+
+HALF = TYPES // 2
+HALF_COLS = HALF * NODES
+HIDDEN_TILES = HIDDEN // P
+
+RUN_BLOCKS = 2
+RUNS = PASSES // RUN_BLOCKS
+
+FLOPS = 2 * FEATURES * HIDDEN * (NODES + NODES * TYPES) + 2 * TYPES * NODES * HIDDEN * REP
+
+
+def tile_attributegnn_pa_k_kernel(
+    tc, image_features, edge_attributes, linear_w, linear_b, fwd_proj, out
+):
+    nc = tc.nc
+    with ExitStack() as ctx:
+        keep = ctx.enter_context(tc.tile_pool(name="keep", bufs=1))
+        raw_pool = ctx.enter_context(tc.tile_pool(name="raw", bufs=RAW_BUFS))
+        grouped_pool = ctx.enter_context(tc.tile_pool(name="grouped", bufs=2 * RUN_BLOCKS))
+        codes_pool = ctx.enter_context(tc.tile_pool(name="codes", bufs=3 * RUN_BLOCKS))
+        small_pool = ctx.enter_context(tc.tile_pool(name="small", bufs=2))
+        acc_pool = ctx.enter_context(tc.psum_pool(name="acc", bufs=1))
+        bank_pool = ctx.enter_context(tc.psum_pool(name="bank", bufs=4))
+        ctx.enter_context(tc.manual_schedule())
+
+        identity = keep.tile([P, P], F32, name="identity")
+        make_identity(nc, identity[:])
+
+        w_rows = linear_w.rearrange("(p t) k -> p t k", t=PACK)
+        order = []
+        views = {}
+        for c in range(CHUNKS):
+            views["w_edge", c] = w_rows[:, :, FEATURES + c * CHUNK : FEATURES + (c + 1) * CHUNK]
+            views["edge_low", c] = edge_attributes[:, 0:HALF, c * CHUNK : (c + 1) * CHUNK]
+            order.extend([("w_edge", c), ("edge_low", c)])
+        views["image", 0] = image_features.rearrange("b (s k) -> b s k", k=CHUNK)
+        order.append(("image", 0))
+        for c in range(CHUNKS):
+            views["w_src", c] = w_rows[:, :, c * CHUNK : (c + 1) * CHUNK]
+            order.append(("w_src", c))
+        views["fwd", 0] = fwd_proj.rearrange("a (p t) r -> p a (t r)", t=PACK)
+        order.append(("fwd", 0))
+        for c in range(CHUNKS):
+            views["edge_high", c] = edge_attributes[:, HALF:TYPES, c * CHUNK : (c + 1) * CHUNK]
+            order.append(("edge_high", c))
+
+        raws = {}
+
+        def load_next(pieces):
+            key = order[len(raws)]
+            raw = raw_pool.tile([P, PACK * CHUNK], BF16, name="raw")
+            raws[key] = raw
+            source = views[key]
+            target = raw[:].rearrange("p (s k) -> p s k", s=source.shape[1])
+            width = source.shape[2] // pieces
+            return [
+                (target[:, :, i * width : (i + 1) * width], source[:, :, i * width : (i + 1) * width])
+                for i in range(pieces)
+            ]
+
+        def start(transfers):
+            for target, source in transfers:
+                nc.sync.dma_start(out=target, in_=source)
+
+        for pair_of_pieces in zip(load_next(CHUNK_PASSES), load_next(CHUNK_PASSES)):
+            start(pair_of_pieces)
+        for i in range(RAW_BUFS - 2):
+            start(load_next(1))
+        bias_bf16 = keep.tile([P, HIDDEN_TILES], BF16, name="bias_bf16")
+        nc.sync.dma_start(out=bias_bf16[:], in_=linear_b.rearrange("(p t) -> p t", t=PACK))
+
+        def words(key):
+            return raws[key][:].bitcast(F32)
+
+        def transpose_block(source_words, first_word, tile_step, first_bank):
+            grouped = grouped_pool.tile([P, PACK * BANK], BF16, name="grouped", align_bytes=64)
+            grouped_words = grouped[:].bitcast(F32)
+            for pair in range(2):
+                bank = bank_pool.tile([P, BANK], F32, name="bank")
+                for quarter in range(4):
+                    s, u = divmod(quarter, 2)
+                    first = first_word + (2 * pair + s) * tile_step + u * P
+                    nc.tensor.transpose(
+                        bank[:, quarter * P : (quarter + 1) * P], source_words[:, first : first + P], identity[:]
+                    )
+                target = grouped_words[:, pair * BANK : (pair + 1) * BANK].rearrange(
+                    "p (s r u) -> p s r u", s=2, u=2
+                )
+                source = bank[:].rearrange("p (s u r) -> p s r u", s=2, u=2)
+                if (first_bank + pair) % 4 == 3:
+                    nc.vector.tensor_copy(out=target, in_=source)
+                else:
+                    nc.scalar.copy(out=target, in_=source)
+            return grouped
+
+        def quantise(grouped, codes, scales):
+            nc.vector.quantize_mx(out=codes.bitcast(FP8X4), scales=scales, in_=grouped)
+
+        def prepare_run(blocks):
+            grouped_tiles = [
+                transpose_block(source_words, first_word, tile_step, 2 * i)
+                for i, (source_words, first_word, tile_step, codes, scales) in enumerate(blocks)
+            ]
+            for grouped, block in zip(grouped_tiles, blocks):
+                quantise(grouped[:], block[3], block[4])
+
+        def new_codes():
+            codes = codes_pool.tile([P, BANK], U32, name="codes", align_bytes=64)
+            scales = codes_pool.tile([P, BANK], U8, name="scales", align_bytes=64)
+            return codes, scales
+
+        def new_accumulators():
+            return [acc_pool.tile([P, BANK], F32, name="acc%d" % t) for t in range(HIDDEN_TILES)]
+
+        def mx(acc, lhs_codes, lhs_scales, rhs_codes, rhs_scales, g):
+            nc.tensor.matmul_mx(
+                out=acc,
+                lhsT=lhs_codes.bitcast(FP8X4),
+                lhsT_scale=lhs_scales,
+                rhs=rhs_codes.bitcast(FP8X4),
+                rhs_scale=rhs_scales,
+                start=(g == 0),
+                stop=(g == PASSES - 1),
+            )
+
+        w_edge_codes = keep.tile([P, PASSES * HIDDEN], U32, name="w_edge_codes", align_bytes=64)
+        w_edge_scales = keep.tile([P, PASSES * HIDDEN], U8, name="w_edge_scales", align_bytes=64)
+        image_codes = keep.tile([P, PASSES * NODES], U32, name="image_codes", align_bytes=64)
+        image_scales = keep.tile([P, PASSES * NODES], U8, name="image_scales", align_bytes=64)
+        fwd_codes = keep.tile([P, TYPES * REP], U32, name="fwd_codes", align_bytes=64)
+        fwd_scales = keep.tile([P, TYPES * REP], U8, name="fwd_scales", align_bytes=64)
+
+        def edge_passes(acc, run):
+            for t in range(HIDDEN_TILES):
+                for g, codes, scales in run:
+                    cols = slice(g * HIDDEN + t * P, g * HIDDEN + (t + 1) * P)
+                    mx(acc[t][:], w_edge_codes[:, cols], w_edge_scales[:, cols], codes[:], scales[:], g)
+
+        def node_passes(acc, run):
+            for t in range(HIDDEN_TILES):
+                for g, codes, scales in run:
+                    cols = slice(t * P, (t + 1) * P)
+                    nodes = slice(g * NODES, (g + 1) * NODES)
+                    mx(acc[t][:, 0:NODES], codes[:, cols], scales[:, cols], image_codes[:, nodes], image_scales[:, nodes], g)
+
+        def prepare_stream(name, n):
+            run = []
+            blocks = []
+            for g in range(n * RUN_BLOCKS, (n + 1) * RUN_BLOCKS):
+                c, g_in_chunk = divmod(g, CHUNK_PASSES)
+                codes, scales = new_codes()
+                run.append((g, codes, scales))
+                blocks.append((words((name, c)), g_in_chunk * PASS_WORDS, CHUNK_WORDS, codes[:], scales[:]))
+            prepare_run(blocks)
+            if (n + 1) * RUN_BLOCKS % CHUNK_PASSES == 0 and len(raws) < len(order):
+                start(load_next(1))
+            return run
+
+        def second_product(agg_grouped, half):
+            agg_codes, agg_scales = new_codes()
+            quantise(agg_grouped[:], agg_codes[:], agg_scales[:])
+            for pair in range(HALF // 2):
+                bank = bank_pool.tile([P, BANK], F32, name="bank")
+                for i in range(2):
+                    a = 2 * pair + i
+                    nodes = slice(a * NODES, (a + 1) * NODES)
+                    reps = slice((half * HALF + a) * REP, (half * HALF + a + 1) * REP)
+                    nc.tensor.matmul_mx(
+                        out=bank[:, i * REP : (i + 1) * REP],
+                        lhsT=agg_codes[:, nodes].bitcast(FP8X4),
+                        lhsT_scale=agg_scales[:, nodes],
+                        rhs=fwd_codes[:, reps].bitcast(FP8X4),
+                        rhs_scale=fwd_scales[:, reps],
+                        start=True,
+                        stop=True,
+                    )
+                result = small_pool.tile([P, BANK], F32, name="result")
+                if pair % 2 == 0:
+                    nc.scalar.copy(out=result[:], in_=bank[:])
+                else:
+                    nc.vector.tensor_copy(out=result[:], in_=bank[:])
+                first_type = half * HALF + 2 * pair
+                nc.sync.dma_start(
+                    out=out[:, first_type : first_type + 2, :], in_=result[:].rearrange("b (a r) -> b a r", a=2)
+                )
+
+        acc = new_accumulators()
+        waiting = None
+        for g in range(PASSES):
+            c, g_in_chunk = divmod(g, CHUNK_PASSES)
+            codes, scales = new_codes()
+            cols = slice(g * HIDDEN, (g + 1) * HIDDEN)
+            prepare_run(
+                [
+                    (words(("w_edge", c)), g_in_chunk * PASS_WORDS, CHUNK_WORDS, w_edge_codes[:, cols], w_edge_scales[:, cols]),
+                    (words(("edge_low", c)), g_in_chunk * PASS_WORDS, CHUNK_WORDS, codes[:], scales[:]),
+                ]
+            )
+            if g_in_chunk == CHUNK_PASSES - 1:
+                start(load_next(1))
+                start(load_next(1))
+            if waiting is not None:
+                edge_passes(acc, waiting)
+            waiting = [(g, codes, scales)]
+
+        def prepare_image(n):
+            blocks = []
+            for j in range(n * RUN_BLOCKS, (n + 1) * RUN_BLOCKS):
+                cols = slice(j * BANK, (j + 1) * BANK)
+                blocks.append((words(("image", 0)), j * PACK * PASS_WORDS, PASS_WORDS, image_codes[:, cols], image_scales[:, cols]))
+            prepare_run(blocks)
+
+        prepare_image(0)
+        edge_passes(acc, waiting)
+        parked = []
+        for t in range(HIDDEN_TILES):
+            park = keep.tile([P, BANK], F32, name="park%d" % t)
+            if t % 2 == 0:
+                nc.scalar.copy(out=park[:], in_=acc[t][:])
+            else:
+                nc.vector.tensor_copy(out=park[:], in_=acc[t][:])
+            parked.append(park)
+        for n in range(1, PASSES // (PACK * RUN_BLOCKS)):
+            prepare_image(n)
+        start(load_next(1))
+
+        acc = new_accumulators()
+        waiting = prepare_stream("w_src", 0)
+        for n in range(1, RUNS):
+            run = prepare_stream("w_src", n)
+            node_passes(acc, waiting)
+            waiting = run
+
+        def prepare_high(n):
+            run = prepare_stream("edge_high", n)
+            for a in range(n * TYPES // RUNS, (n + 1) * TYPES // RUNS):
+                fwd_grouped = small_pool.tile([P, PACK * REP], BF16, name="fwd_grouped", align_bytes=64)
+                nc.scalar.copy(
+                    out=fwd_grouped[:].rearrange("p (r t) -> p r t", t=PACK),
+                    in_=raws["fwd", 0][:, a * PACK * REP : (a + 1) * PACK * REP].rearrange("p (t r) -> p r t", t=PACK),
+                )
+                reps = slice(a * REP, (a + 1) * REP)
+                quantise(fwd_grouped[:], fwd_codes[:, reps], fwd_scales[:, reps])
+            return run
+
+        run = prepare_high(0)
+        node_passes(acc, waiting)
+        waiting = run
+
+        bias = keep.tile([P, HIDDEN_TILES], F32, name="bias")
+        nc.vector.tensor_copy(out=bias[:], in_=bias_bf16[:])
+        node_bias = keep.tile([P, HIDDEN_TILES * NODES], F32, name="node_bias")
+        for t in range(HIDDEN_TILES):
+            nc.scalar.activation(
+                out=node_bias[:, t * NODES : (t + 1) * NODES],
+                in_=acc[t][:, 0:NODES],
+                func=mybir.ActivationFunctionType.Identity,
+                bias=bias[:, t : t + 1],
+            )
+
+        def node_bias_for_all_types(t):
+            return node_bias[:, t * NODES : (t + 1) * NODES].unsqueeze(1).to_broadcast([P, HALF, NODES])
+
+        agg_low = keep.tile([P, PACK * HALF_COLS], BF16, name="agg_low", align_bytes=64)
+        for t in range(HIDDEN_TILES):
+            nc.gpsimd.tensor_tensor(
+                out=agg_low[:].rearrange("p (a b t) -> p t a b", a=HALF, t=PACK)[:, t],
+                in0=parked[t][:].rearrange("p (a b) -> p a b", a=HALF),
+                in1=node_bias_for_all_types(t),
+                op=mybir.AluOpType.add,
+            )
+
+        acc = new_accumulators()
+        for n in range(1, RUNS):
+            run = prepare_high(n)
+            edge_passes(acc, waiting)
+            waiting = run
+        second_product(agg_low, 0)
+        edge_passes(acc, waiting)
+
+        agg_rows = keep.tile([P, PACK * HALF_COLS], BF16, name="agg_rows")
+        for t in range(HIDDEN_TILES):
+            nc.vector.tensor_tensor(
+                out=agg_rows[:, t * HALF_COLS : (t + 1) * HALF_COLS].rearrange("p (a b) -> p a b", a=HALF),
+                in0=acc[t][:].rearrange("p (a b) -> p a b", a=HALF),
+                in1=node_bias_for_all_types(t),
+                op=mybir.AluOpType.add,
+            )
+        agg_high = keep.tile([P, PACK * HALF_COLS], BF16, name="agg_high", align_bytes=64)
+        nc.vector.tensor_copy(
+            out=agg_high[:].rearrange("p (c t) -> p c t", t=PACK),
+            in_=agg_rows[:].rearrange("p (t c) -> p c t", t=PACK),
+        )
+        second_product(agg_high, 1)

@@ -34,6 +34,7 @@ HIDDEN_TILES = HIDDEN // P
 
 RUN_BLOCKS = 2
 RUNS = PASSES // RUN_BLOCKS
+LOW_RUN = RUN_BLOCKS // 2
 
 FLOPS = 2 * FEATURES * HIDDEN * (NODES + NODES * TYPES) + 2 * TYPES * NODES * HIDDEN * REP
 
@@ -74,18 +75,17 @@ def tile_attributegnn_pa_k_kernel(
             order.append(("edge_high", c))
 
         raws = {}
+        pieces_of = {}
 
         def load_next(pieces):
             key = order[len(raws)]
             raw = raw_pool.tile([P, PACK * CHUNK], BF16, name="raw")
             raws[key] = raw
+            pieces_of[key] = pieces
             source = views[key]
-            target = raw[:].rearrange("p (s k) -> p s k", s=source.shape[1])
+            target = raw[:].rearrange("p (i s k) -> p i s k", i=pieces, s=source.shape[1])
             width = source.shape[2] // pieces
-            return [
-                (target[:, :, i * width : (i + 1) * width], source[:, :, i * width : (i + 1) * width])
-                for i in range(pieces)
-            ]
+            return [(target[:, i], source[:, :, i * width : (i + 1) * width]) for i in range(pieces)]
 
         def start(transfers):
             for target, source in transfers:
@@ -98,8 +98,11 @@ def tile_attributegnn_pa_k_kernel(
         bias_bf16 = keep.tile([P, HIDDEN_TILES], BF16, name="bias_bf16")
         nc.sync.dma_start(out=bias_bf16[:], in_=linear_b.rearrange("(p t) -> p t", t=PACK))
 
-        def words(key):
-            return raws[key][:].bitcast(F32)
+        def tiles_of_pass(key, g_in_chunk):
+            passes_in_piece = CHUNK_PASSES // pieces_of[key]
+            piece, g_in_piece = divmod(g_in_chunk, passes_in_piece)
+            tile_step = passes_in_piece * PASS_WORDS
+            return raws[key][:].bitcast(F32), piece * PACK * tile_step + g_in_piece * PASS_WORDS, tile_step
 
         def transpose_block(source_words, first_word, tile_step, first_bank):
             grouped = grouped_pool.tile([P, PACK * BANK], BF16, name="grouped", align_bytes=64)
@@ -125,25 +128,31 @@ def tile_attributegnn_pa_k_kernel(
         def quantise(grouped, codes, scales):
             nc.vector.quantize_mx(out=codes.bitcast(FP8X4), scales=scales, in_=grouped)
 
-        def prepare_run(blocks):
+        history = []
+
+        def advance(blocks, passes):
+            n = len(history)
+            if n >= 1:
+                for grouped, block in zip(history[n - 1][0], history[n - 1][1]):
+                    quantise(grouped[:], block[3], block[4])
             grouped_tiles = [
-                transpose_block(source_words, first_word, tile_step, 2 * i)
-                for i, (source_words, first_word, tile_step, codes, scales) in enumerate(blocks)
+                transpose_block(block[0], block[1], block[2], 2 * i) for i, block in enumerate(blocks)
             ]
-            for grouped, block in zip(grouped_tiles, blocks):
-                quantise(grouped[:], block[3], block[4])
+            history.append((grouped_tiles, blocks, passes))
+            if n >= 2 and history[n - 2][2] is not None:
+                history[n - 2][2]()
+
+        def later(passes, run):
+            return lambda: passes(run)
 
         def new_codes():
             codes = codes_pool.tile([P, BANK], U32, name="codes", align_bytes=64)
             scales = codes_pool.tile([P, BANK], U8, name="scales", align_bytes=64)
             return codes, scales
 
-        def new_accumulators():
-            return [acc_pool.tile([P, BANK], F32, name="acc%d" % t) for t in range(HIDDEN_TILES)]
-
-        def mx(acc, lhs_codes, lhs_scales, rhs_codes, rhs_scales, g):
+        def mx(bank, lhs_codes, lhs_scales, rhs_codes, rhs_scales, g):
             nc.tensor.matmul_mx(
-                out=acc,
+                out=bank,
                 lhsT=lhs_codes.bitcast(FP8X4),
                 lhsT_scale=lhs_scales,
                 rhs=rhs_codes.bitcast(FP8X4),
@@ -159,31 +168,21 @@ def tile_attributegnn_pa_k_kernel(
         fwd_codes = keep.tile([P, TYPES * REP], U32, name="fwd_codes", align_bytes=64)
         fwd_scales = keep.tile([P, TYPES * REP], U8, name="fwd_scales", align_bytes=64)
 
-        def edge_passes(acc, run):
+        acc = {}
+
+        def open_banks(name, run):
+            if run[0][0] == 0:
+                acc[name] = [acc_pool.tile([P, BANK], F32, name="acc%d" % t) for t in range(HIDDEN_TILES)]
+
+        def is_last(run):
+            return run[-1][0] == PASSES - 1
+
+        def edge_passes(name, run):
+            open_banks(name, run)
             for t in range(HIDDEN_TILES):
                 for g, codes, scales in run:
                     cols = slice(g * HIDDEN + t * P, g * HIDDEN + (t + 1) * P)
-                    mx(acc[t][:], w_edge_codes[:, cols], w_edge_scales[:, cols], codes[:], scales[:], g)
-
-        def node_passes(acc, run):
-            for t in range(HIDDEN_TILES):
-                for g, codes, scales in run:
-                    cols = slice(t * P, (t + 1) * P)
-                    nodes = slice(g * NODES, (g + 1) * NODES)
-                    mx(acc[t][:, 0:NODES], codes[:, cols], scales[:, cols], image_codes[:, nodes], image_scales[:, nodes], g)
-
-        def prepare_stream(name, n):
-            run = []
-            blocks = []
-            for g in range(n * RUN_BLOCKS, (n + 1) * RUN_BLOCKS):
-                c, g_in_chunk = divmod(g, CHUNK_PASSES)
-                codes, scales = new_codes()
-                run.append((g, codes, scales))
-                blocks.append((words((name, c)), g_in_chunk * PASS_WORDS, CHUNK_WORDS, codes[:], scales[:]))
-            prepare_run(blocks)
-            if (n + 1) * RUN_BLOCKS % CHUNK_PASSES == 0 and len(raws) < len(order):
-                start(load_next(1))
-            return run
+                    mx(acc[name][t][:], w_edge_codes[:, cols], w_edge_scales[:, cols], codes[:], scales[:], g)
 
         def second_product(agg_grouped, half):
             agg_codes, agg_scales = new_codes()
@@ -213,111 +212,128 @@ def tile_attributegnn_pa_k_kernel(
                     out=out[:, first_type : first_type + 2, :], in_=result[:].rearrange("b (a r) -> b a r", a=2)
                 )
 
-        acc = new_accumulators()
-        waiting = None
-        for g in range(PASSES):
-            c, g_in_chunk = divmod(g, CHUNK_PASSES)
-            codes, scales = new_codes()
-            cols = slice(g * HIDDEN, (g + 1) * HIDDEN)
-            prepare_run(
-                [
-                    (words(("w_edge", c)), g_in_chunk * PASS_WORDS, CHUNK_WORDS, w_edge_codes[:, cols], w_edge_scales[:, cols]),
-                    (words(("edge_low", c)), g_in_chunk * PASS_WORDS, CHUNK_WORDS, codes[:], scales[:]),
-                ]
-            )
-            if g_in_chunk == CHUNK_PASSES - 1:
-                start(load_next(1))
-                start(load_next(1))
-            if waiting is not None:
-                edge_passes(acc, waiting)
-            waiting = [(g, codes, scales)]
+        parked = [keep.tile([P, BANK], F32, name="park%d" % t) for t in range(HIDDEN_TILES)]
 
-        def prepare_image(n):
-            blocks = []
-            for j in range(n * RUN_BLOCKS, (n + 1) * RUN_BLOCKS):
-                cols = slice(j * BANK, (j + 1) * BANK)
-                blocks.append((words(("image", 0)), j * PACK * PASS_WORDS, PASS_WORDS, image_codes[:, cols], image_scales[:, cols]))
-            prepare_run(blocks)
-
-        prepare_image(0)
-        edge_passes(acc, waiting)
-        parked = []
-        for t in range(HIDDEN_TILES):
-            park = keep.tile([P, BANK], F32, name="park%d" % t)
-            if t % 2 == 0:
-                nc.scalar.copy(out=park[:], in_=acc[t][:])
-            else:
-                nc.vector.tensor_copy(out=park[:], in_=acc[t][:])
-            parked.append(park)
-        for n in range(1, PASSES // (PACK * RUN_BLOCKS)):
-            prepare_image(n)
-        start(load_next(1))
-
-        acc = new_accumulators()
-        waiting = prepare_stream("w_src", 0)
-        for n in range(1, RUNS):
-            run = prepare_stream("w_src", n)
-            node_passes(acc, waiting)
-            waiting = run
-
-        def prepare_high(n):
-            run = prepare_stream("edge_high", n)
-            for a in range(n * TYPES // RUNS, (n + 1) * TYPES // RUNS):
-                fwd_grouped = small_pool.tile([P, PACK * REP], BF16, name="fwd_grouped", align_bytes=64)
-                nc.scalar.copy(
-                    out=fwd_grouped[:].rearrange("p (r t) -> p r t", t=PACK),
-                    in_=raws["fwd", 0][:, a * PACK * REP : (a + 1) * PACK * REP].rearrange("p (t r) -> p r t", t=PACK),
-                )
-                reps = slice(a * REP, (a + 1) * REP)
-                quantise(fwd_grouped[:], fwd_codes[:, reps], fwd_scales[:, reps])
-            return run
-
-        run = prepare_high(0)
-        node_passes(acc, waiting)
-        waiting = run
+        def low_passes(run):
+            edge_passes("low", run)
+            if is_last(run):
+                for t in range(HIDDEN_TILES):
+                    if t % 2 == 0:
+                        nc.scalar.copy(out=parked[t][:], in_=acc["low"][t][:])
+                    else:
+                        nc.vector.tensor_copy(out=parked[t][:], in_=acc["low"][t][:])
 
         bias = keep.tile([P, HIDDEN_TILES], F32, name="bias")
-        nc.vector.tensor_copy(out=bias[:], in_=bias_bf16[:])
         node_bias = keep.tile([P, HIDDEN_TILES * NODES], F32, name="node_bias")
-        for t in range(HIDDEN_TILES):
-            nc.scalar.activation(
-                out=node_bias[:, t * NODES : (t + 1) * NODES],
-                in_=acc[t][:, 0:NODES],
-                func=mybir.ActivationFunctionType.Identity,
-                bias=bias[:, t : t + 1],
-            )
+        agg_low = keep.tile([P, PACK * HALF_COLS], BF16, name="agg_low", align_bytes=64)
 
         def node_bias_for_all_types(t):
             return node_bias[:, t * NODES : (t + 1) * NODES].unsqueeze(1).to_broadcast([P, HALF, NODES])
 
-        agg_low = keep.tile([P, PACK * HALF_COLS], BF16, name="agg_low", align_bytes=64)
-        for t in range(HIDDEN_TILES):
-            nc.gpsimd.tensor_tensor(
-                out=agg_low[:].rearrange("p (a b t) -> p t a b", a=HALF, t=PACK)[:, t],
-                in0=parked[t][:].rearrange("p (a b) -> p a b", a=HALF),
-                in1=node_bias_for_all_types(t),
-                op=mybir.AluOpType.add,
-            )
-
-        acc = new_accumulators()
-        for n in range(1, RUNS):
-            run = prepare_high(n)
-            edge_passes(acc, waiting)
-            waiting = run
-        second_product(agg_low, 0)
-        edge_passes(acc, waiting)
+        def node_passes(run):
+            open_banks("node", run)
+            for t in range(HIDDEN_TILES):
+                for g, codes, scales in run:
+                    cols = slice(t * P, (t + 1) * P)
+                    nodes = slice(g * NODES, (g + 1) * NODES)
+                    mx(
+                        acc["node"][t][:, 0:NODES],
+                        codes[:, cols],
+                        scales[:, cols],
+                        image_codes[:, nodes],
+                        image_scales[:, nodes],
+                        g,
+                    )
+            if is_last(run):
+                nc.vector.tensor_copy(out=bias[:], in_=bias_bf16[:])
+                for t in range(HIDDEN_TILES):
+                    nc.scalar.activation(
+                        out=node_bias[:, t * NODES : (t + 1) * NODES],
+                        in_=acc["node"][t][:, 0:NODES],
+                        func=mybir.ActivationFunctionType.Identity,
+                        bias=bias[:, t : t + 1],
+                    )
+                for t in range(HIDDEN_TILES):
+                    nc.gpsimd.tensor_tensor(
+                        out=agg_low[:].rearrange("p (a b t) -> p t a b", a=HALF, t=PACK)[:, t],
+                        in0=parked[t][:].rearrange("p (a b) -> p a b", a=HALF),
+                        in1=node_bias_for_all_types(t),
+                        op=mybir.AluOpType.add,
+                    )
 
         agg_rows = keep.tile([P, PACK * HALF_COLS], BF16, name="agg_rows")
-        for t in range(HIDDEN_TILES):
-            nc.vector.tensor_tensor(
-                out=agg_rows[:, t * HALF_COLS : (t + 1) * HALF_COLS].rearrange("p (a b) -> p a b", a=HALF),
-                in0=acc[t][:].rearrange("p (a b) -> p a b", a=HALF),
-                in1=node_bias_for_all_types(t),
-                op=mybir.AluOpType.add,
-            )
         agg_high = keep.tile([P, PACK * HALF_COLS], BF16, name="agg_high", align_bytes=64)
-        nc.vector.tensor_copy(
-            out=agg_high[:].rearrange("p (c t) -> p c t", t=PACK),
-            in_=agg_rows[:].rearrange("p (t c) -> p c t", t=PACK),
-        )
-        second_product(agg_high, 1)
+
+        def high_passes(run):
+            if is_last(run):
+                second_product(agg_low, 0)
+            edge_passes("high", run)
+            if is_last(run):
+                for t in range(HIDDEN_TILES):
+                    nc.vector.tensor_tensor(
+                        out=agg_rows[:, t * HALF_COLS : (t + 1) * HALF_COLS].rearrange("p (a b) -> p a b", a=HALF),
+                        in0=acc["high"][t][:].rearrange("p (a b) -> p a b", a=HALF),
+                        in1=node_bias_for_all_types(t),
+                        op=mybir.AluOpType.add,
+                    )
+                nc.vector.tensor_copy(
+                    out=agg_high[:].rearrange("p (c t) -> p c t", t=PACK),
+                    in_=agg_rows[:].rearrange("p (t c) -> p c t", t=PACK),
+                )
+                second_product(agg_high, 1)
+
+        def stream_run(name, n, passes):
+            run = []
+            blocks = []
+            for g in range(n * RUN_BLOCKS, (n + 1) * RUN_BLOCKS):
+                c, g_in_chunk = divmod(g, CHUNK_PASSES)
+                codes, scales = new_codes()
+                run.append((g, codes, scales))
+                blocks.append(tiles_of_pass((name, c), g_in_chunk) + (codes[:], scales[:]))
+            advance(blocks, later(passes, run))
+            if (n + 1) * RUN_BLOCKS % CHUNK_PASSES == 0 and len(raws) < len(order):
+                start(load_next(1))
+
+        for n in range(PASSES // LOW_RUN):
+            run = []
+            blocks = []
+            for g in range(n * LOW_RUN, (n + 1) * LOW_RUN):
+                c, g_in_chunk = divmod(g, CHUNK_PASSES)
+                codes, scales = new_codes()
+                run.append((g, codes, scales))
+                cols = slice(g * HIDDEN, (g + 1) * HIDDEN)
+                blocks.append(tiles_of_pass(("w_edge", c), g_in_chunk) + (w_edge_codes[:, cols], w_edge_scales[:, cols]))
+                blocks.append(tiles_of_pass(("edge_low", c), g_in_chunk) + (codes[:], scales[:]))
+            advance(blocks, later(low_passes, run))
+            if (n + 1) * LOW_RUN % CHUNK_PASSES == 0:
+                start(load_next(1))
+                start(load_next(1))
+
+        image_words = raws["image", 0][:].bitcast(F32)
+        for n in range(PASSES // (PACK * RUN_BLOCKS)):
+            blocks = []
+            for j in range(n * RUN_BLOCKS, (n + 1) * RUN_BLOCKS):
+                cols = slice(j * BANK, (j + 1) * BANK)
+                blocks.append((image_words, j * PACK * PASS_WORDS, PASS_WORDS, image_codes[:, cols], image_scales[:, cols]))
+            advance(blocks, None)
+        start(load_next(1))
+
+        for n in range(RUNS):
+            stream_run("w_src", n, node_passes)
+
+        for n in range(RUNS):
+            types_of_run = range(n * TYPES // RUNS, (n + 1) * TYPES // RUNS)
+            fwd_grouped = {}
+            for a in types_of_run:
+                fwd_grouped[a] = small_pool.tile([P, PACK * REP], BF16, name="fwd_grouped", align_bytes=64)
+                nc.scalar.copy(
+                    out=fwd_grouped[a][:].rearrange("p (r t) -> p r t", t=PACK),
+                    in_=raws["fwd", 0][:, a * PACK * REP : (a + 1) * PACK * REP].rearrange("p (t r) -> p r t", t=PACK),
+                )
+            stream_run("edge_high", n, high_passes)
+            for a in types_of_run:
+                reps = slice(a * REP, (a + 1) * REP)
+                quantise(fwd_grouped[a][:], fwd_codes[:, reps], fwd_scales[:, reps])
+
+        advance([], None)
+        advance([], None)

@@ -59,6 +59,7 @@ def tile_attributegnn_pa_k_kernel(
         w_rows = linear_w.rearrange("(p t) k -> p t k", t=PACK)
         order = []
         views = {}
+        pieces_of = {}
         for c in range(CHUNKS):
             views["w_edge", c] = w_rows[:, :, FEATURES + c * CHUNK : FEATURES + (c + 1) * CHUNK]
             views["edge_low", c] = edge_attributes[:, 0:HALF, c * CHUNK : (c + 1) * CHUNK]
@@ -69,32 +70,36 @@ def tile_attributegnn_pa_k_kernel(
             views["w_src", c] = w_rows[:, :, c * CHUNK : (c + 1) * CHUNK]
             order.append(("w_src", c))
         views["fwd", 0] = fwd_proj.rearrange("a (p t) r -> p a (t r)", t=PACK)
-        order.append(("fwd", 0))
         for c in range(CHUNKS):
+            if c == CHUNKS // 2:
+                order.append(("fwd", 0))
             views["edge_high", c] = edge_attributes[:, HALF:TYPES, c * CHUNK : (c + 1) * CHUNK]
             order.append(("edge_high", c))
+        for key in order:
+            pieces_of[key] = 1
+        for c in range(CHUNKS):
+            for name in ("w_edge", "edge_low"):
+                pieces_of[name, c] = CHUNK_PASSES if c == 0 else CHUNK_PASSES // 2
 
         raws = {}
-        pieces_of = {}
 
-        def load_next(pieces):
+        def load_next():
             key = order[len(raws)]
             raw = raw_pool.tile([P, PACK * CHUNK], BF16, name="raw")
             raws[key] = raw
-            pieces_of[key] = pieces
+            pieces = pieces_of[key]
             source = views[key]
             target = raw[:].rearrange("p (i s k) -> p i s k", i=pieces, s=source.shape[1])
             width = source.shape[2] // pieces
             return [(target[:, i], source[:, :, i * width : (i + 1) * width]) for i in range(pieces)]
 
-        def start(transfers):
-            for target, source in transfers:
-                nc.sync.dma_start(out=target, in_=source)
+        def refill(count):
+            for pieces_read_together in zip(*[load_next() for i in range(count)]):
+                for target, source in pieces_read_together:
+                    nc.sync.dma_start(out=target, in_=source)
 
-        for pair_of_pieces in zip(load_next(CHUNK_PASSES), load_next(CHUNK_PASSES)):
-            start(pair_of_pieces)
-        for i in range(RAW_BUFS - 2):
-            start(load_next(1))
+        for i in range(RAW_BUFS // 2):
+            refill(2)
         bias_bf16 = keep.tile([P, HIDDEN_TILES], BF16, name="bias_bf16")
         nc.sync.dma_start(out=bias_bf16[:], in_=linear_b.rearrange("(p t) -> p t", t=PACK))
 
@@ -292,7 +297,7 @@ def tile_attributegnn_pa_k_kernel(
                 blocks.append(tiles_of_pass((name, c), g_in_chunk) + (codes[:], scales[:]))
             advance(blocks, later(passes, run))
             if (n + 1) * RUN_BLOCKS % CHUNK_PASSES == 0 and len(raws) < len(order):
-                start(load_next(1))
+                refill(1)
 
         for n in range(PASSES // LOW_RUN):
             run = []
@@ -306,8 +311,7 @@ def tile_attributegnn_pa_k_kernel(
                 blocks.append(tiles_of_pass(("edge_low", c), g_in_chunk) + (codes[:], scales[:]))
             advance(blocks, later(low_passes, run))
             if (n + 1) * LOW_RUN % CHUNK_PASSES == 0:
-                start(load_next(1))
-                start(load_next(1))
+                refill(2)
 
         image_words = raws["image", 0][:].bitcast(F32)
         for n in range(PASSES // (PACK * RUN_BLOCKS)):
@@ -316,20 +320,23 @@ def tile_attributegnn_pa_k_kernel(
                 cols = slice(j * BANK, (j + 1) * BANK)
                 blocks.append((image_words, j * PACK * PASS_WORDS, PASS_WORDS, image_codes[:, cols], image_scales[:, cols]))
             advance(blocks, None)
-        start(load_next(1))
+        refill(1)
 
         for n in range(RUNS):
             stream_run("w_src", n, node_passes)
 
         for n in range(RUNS):
-            types_of_run = range(n * TYPES // RUNS, (n + 1) * TYPES // RUNS)
+            m = n - RUNS // 2
+            types_of_run = range(m * 2 * TYPES // RUNS, (m + 1) * 2 * TYPES // RUNS) if m >= 0 else range(0)
             fwd_grouped = {}
             for a in types_of_run:
                 fwd_grouped[a] = small_pool.tile([P, PACK * REP], BF16, name="fwd_grouped", align_bytes=64)
-                nc.scalar.copy(
-                    out=fwd_grouped[a][:].rearrange("p (r t) -> p r t", t=PACK),
-                    in_=raws["fwd", 0][:, a * PACK * REP : (a + 1) * PACK * REP].rearrange("p (t r) -> p r t", t=PACK),
-                )
+                target = fwd_grouped[a][:].rearrange("p (r t) -> p r t", t=PACK)
+                source = raws["fwd", 0][:, a * PACK * REP : (a + 1) * PACK * REP].rearrange("p (t r) -> p r t", t=PACK)
+                if a % 2 == 0:
+                    nc.scalar.copy(out=target, in_=source)
+                else:
+                    nc.vector.tensor_copy(out=target, in_=source)
             stream_run("edge_high", n, high_passes)
             for a in types_of_run:
                 reps = slice(a * REP, (a + 1) * REP)

from contextlib import ExitStack

import concourse.mybir as mybir
from concourse.masks import make_identity

F32 = mybir.dt.float32
BF16 = mybir.dt.bfloat16
U32 = mybir.dt.uint32
U8 = mybir.dt.uint8
FP8X4 = mybir.dt.float8_e4m3fn_x4

NODES = 128
TYPES = 8
FEATURES = 8192
HIDDEN = 512
REP = 256

P = 128
PACK = 4
K_PASS = P * PACK
PASSES = FEATURES // K_PASS
PASS_WORDS = K_PASS // 2
BANK = 512

CHUNK_PASSES = 4
CHUNK = CHUNK_PASSES * K_PASS
CHUNKS = FEATURES // CHUNK
CHUNK_WORDS = CHUNK // 2
RAW_BUFS = 6

HALF = TYPES // 2
HALF_COLS = HALF * NODES
HIDDEN_TILES = HIDDEN // P

RUN_BLOCKS = 2
RUNS = PASSES // RUN_BLOCKS
LOW_RUN = RUN_BLOCKS // 2

FLOPS = 2 * FEATURES * HIDDEN * (NODES + NODES * TYPES) + 2 * TYPES * NODES * HIDDEN * REP


def tile_attributegnn_pa_k_kernel(
    tc, image_features, edge_attributes, linear_w, linear_b, fwd_proj, out
):
    nc = tc.nc
    with ExitStack() as ctx:
        keep = ctx.enter_context(tc.tile_pool(name="keep", bufs=1))
        raw_pool = ctx.enter_context(tc.tile_pool(name="raw", bufs=RAW_BUFS))
        grouped_pool = ctx.enter_context(tc.tile_pool(name="grouped", bufs=2 * RUN_BLOCKS))
        codes_pool = ctx.enter_context(tc.tile_pool(name="codes", bufs=3 * RUN_BLOCKS))
        small_pool = ctx.enter_context(tc.tile_pool(name="small", bufs=2))
        acc_pool = ctx.enter_context(tc.psum_pool(name="acc", bufs=1))
        bank_pool = ctx.enter_context(tc.psum_pool(name="bank", bufs=4))
        ctx.enter_context(tc.manual_schedule())

        identity = keep.tile([P, P], F32, name="identity")
        make_identity(nc, identity[:])

        w_rows = linear_w.rearrange("(p t) k -> p t k", t=PACK)
        order = []
        views = {}
        pieces_of = {}
        for c in range(CHUNKS):
            views["w_edge", c] = w_rows[:, :, FEATURES + c * CHUNK : FEATURES + (c + 1) * CHUNK]
            views["edge_low", c] = edge_attributes[:, 0:HALF, c * CHUNK : (c + 1) * CHUNK]
            order.extend([("w_edge", c), ("edge_low", c)])
        views["image", 0] = image_features.rearrange("b (s k) -> b s k", k=CHUNK)
        order.append(("image", 0))
        for c in range(CHUNKS):
            views["w_src", c] = w_rows[:, :, c * CHUNK : (c + 1) * CHUNK]
            order.append(("w_src", c))
        views["fwd", 0] = fwd_proj.rearrange("a (p t) r -> p a (t r)", t=PACK)
        for c in range(CHUNKS):
            if c == CHUNKS // 2:
                order.append(("fwd", 0))
            views["edge_high", c] = edge_attributes[:, HALF:TYPES, c * CHUNK : (c + 1) * CHUNK]
            order.append(("edge_high", c))
        for key in order:
            pieces_of[key] = 1
        for c in range(CHUNKS):
            for name in ("w_edge", "edge_low"):
                pieces_of[name, c] = CHUNK_PASSES if c == 0 else CHUNK_PASSES // 2

        raws = {}

        def load_next():
            key = order[len(raws)]
            raw = raw_pool.tile([P, PACK * CHUNK], BF16, name="raw")
            raws[key] = raw
            pieces = pieces_of[key]
            source = views[key]
            target = raw[:].rearrange("p (i s k) -> p i s k", i=pieces, s=source.shape[1])
            width = source.shape[2] // pieces
            return [(target[:, i], source[:, :, i * width : (i + 1) * width]) for i in range(pieces)]

        def refill(count):
            for pieces_read_together in zip(*[load_next() for i in range(count)]):
                for target, source in pieces_read_together:
                    nc.sync.dma_start(out=target, in_=source)

        for i in range(RAW_BUFS // 2):
            refill(2)
        bias_bf16 = keep.tile([P, HIDDEN_TILES], BF16, name="bias_bf16")
        nc.sync.dma_start(out=bias_bf16[:], in_=linear_b.rearrange("(p t) -> p t", t=PACK))

        def tiles_of_pass(key, g_in_chunk):
            passes_in_piece = CHUNK_PASSES // pieces_of[key]
            piece, g_in_piece = divmod(g_in_chunk, passes_in_piece)
            tile_step = passes_in_piece * PASS_WORDS
            return raws[key][:].bitcast(F32), piece * PACK * tile_step + g_in_piece * PASS_WORDS, tile_step

        def transpose_block(source_words, first_word, tile_step, first_bank):
            grouped = grouped_pool.tile([P, PACK * BANK], BF16, name="grouped", align_bytes=64)
            grouped_words = grouped[:].bitcast(F32)
            for pair in range(2):
                bank = bank_pool.tile([P, BANK], F32, name="bank")
                for quarter in range(4):
                    s, u = divmod(quarter, 2)
                    first = first_word + (2 * pair + s) * tile_step + u * P
                    nc.tensor.transpose(
                        bank[:, quarter * P : (quarter + 1) * P], source_words[:, first : first + P], identity[:]
                    )
                target = grouped_words[:, pair * BANK : (pair + 1) * BANK].rearrange(
                    "p (s r u) -> p s r u", s=2, u=2
                )
                source = bank[:].rearrange("p (s u r) -> p s r u", s=2, u=2)
                if (first_bank + pair) % 4 == 3:
                    nc.vector.tensor_copy(out=target, in_=source)
                else:
                    nc.scalar.copy(out=target, in_=source)
            return grouped

        def quantise(grouped, codes, scales):
            nc.vector.quantize_mx(out=codes.bitcast(FP8X4), scales=scales, in_=grouped)

        history = []

        def advance(blocks, passes):
            n = len(history)
            if n >= 1:
                for grouped, block in zip(history[n - 1][0], history[n - 1][1]):
                    quantise(grouped[:], block[3], block[4])
            grouped_tiles = [
                transpose_block(block[0], block[1], block[2], 2 * i) for i, block in enumerate(blocks)
            ]
            history.append((grouped_tiles, blocks, passes))
            if n >= 2 and history[n - 2][2] is not None:
                history[n - 2][2]()

        def later(passes, run):
            return lambda: passes(run)

        def new_codes():
            codes = codes_pool.tile([P, BANK], U32, name="codes", align_bytes=64)
            scales = codes_pool.tile([P, BANK], U8, name="scales", align_bytes=64)
            return codes, scales

        def mx(bank, lhs_codes, lhs_scales, rhs_codes, rhs_scales, g):
            nc.tensor.matmul_mx(
                out=bank,
                lhsT=lhs_codes.bitcast(FP8X4),
                lhsT_scale=lhs_scales,
                rhs=rhs_codes.bitcast(FP8X4),
                rhs_scale=rhs_scales,
                start=(g == 0),
                stop=(g == PASSES - 1),
            )

        w_edge_codes = keep.tile([P, PASSES * HIDDEN], U32, name="w_edge_codes", align_bytes=64)
        w_edge_scales = keep.tile([P, PASSES * HIDDEN], U8, name="w_edge_scales", align_bytes=64)
        image_codes = keep.tile([P, PASSES * NODES], U32, name="image_codes", align_bytes=64)
        image_scales = keep.tile([P, PASSES * NODES], U8, name="image_scales", align_bytes=64)
        fwd_codes = keep.tile([P, TYPES * REP], U32, name="fwd_codes", align_bytes=64)
        fwd_scales = keep.tile([P, TYPES * REP], U8, name="fwd_scales", align_bytes=64)

        acc = {}

        def open_banks(name, run):
            if run[0][0] == 0:
                acc[name] = [acc_pool.tile([P, BANK], F32, name="acc%d" % t) for t in range(HIDDEN_TILES)]

        def is_last(run):
            return run[-1][0] == PASSES - 1

        def edge_passes(name, run):
            open_banks(name, run)
            for t in range(HIDDEN_TILES):
                for g, codes, scales in run:
                    cols = slice(g * HIDDEN + t * P, g * HIDDEN + (t + 1) * P)
                    mx(acc[name][t][:], w_edge_codes[:, cols], w_edge_scales[:, cols], codes[:], scales[:], g)

        def second_product(agg_grouped, half):
            agg_codes, agg_scales = new_codes()
            quantise(agg_grouped[:], agg_codes[:], agg_scales[:])
            for pair in range(HALF // 2):
                bank = bank_pool.tile([P, BANK], F32, name="bank")
                for i in range(2):
                    a = 2 * pair + i
                    nodes = slice(a * NODES, (a + 1) * NODES)
                    reps = slice((half * HALF + a) * REP, (half * HALF + a + 1) * REP)
                    nc.tensor.matmul_mx(
                        out=bank[:, i * REP : (i + 1) * REP],
                        lhsT=agg_codes[:, nodes].bitcast(FP8X4),
                        lhsT_scale=agg_scales[:, nodes],
                        rhs=fwd_codes[:, reps].bitcast(FP8X4),
                        rhs_scale=fwd_scales[:, reps],
                        start=True,
                        stop=True,
                    )
                result = small_pool.tile([P, BANK], F32, name="result")
                if pair % 2 == 0:
                    nc.scalar.copy(out=result[:], in_=bank[:])
                else:
                    nc.vector.tensor_copy(out=result[:], in_=bank[:])
                first_type = half * HALF + 2 * pair
                nc.sync.dma_start(
                    out=out[:, first_type : first_type + 2, :], in_=result[:].rearrange("b (a r) -> b a r", a=2)
                )

        parked = [keep.tile([P, BANK], F32, name="park%d" % t) for t in range(HIDDEN_TILES)]

        def low_passes(run):
            edge_passes("low", run)
            if is_last(run):
                for t in range(HIDDEN_TILES):
                    if t % 2 == 0:
                        nc.scalar.copy(out=parked[t][:], in_=acc["low"][t][:])
                    else:
                        nc.vector.tensor_copy(out=parked[t][:], in_=acc["low"][t][:])

        bias = keep.tile([P, HIDDEN_TILES], F32, name="bias")
        node_bias = keep.tile([P, HIDDEN_TILES * NODES], F32, name="node_bias")
        agg_low = keep.tile([P, PACK * HALF_COLS], BF16, name="agg_low", align_bytes=64)

        def node_bias_for_all_types(t):
            return node_bias[:, t * NODES : (t + 1) * NODES].unsqueeze(1).to_broadcast([P, HALF, NODES])

        def node_passes(run):
            open_banks("node", run)
            for t in range(HIDDEN_TILES):
                for g, codes, scales in run:
                    cols = slice(t * P, (t + 1) * P)
                    nodes = slice(g * NODES, (g + 1) * NODES)
                    mx(
                        acc["node"][t][:, 0:NODES],
                        codes[:, cols],
                        scales[:, cols],
                        image_codes[:, nodes],
                        image_scales[:, nodes],
                        g,
                    )
            if is_last(run):
                nc.vector.tensor_copy(out=bias[:], in_=bias_bf16[:])
                for t in range(HIDDEN_TILES):
                    nc.scalar.activation(
                        out=node_bias[:, t * NODES : (t + 1) * NODES],
                        in_=acc["node"][t][:, 0:NODES],
                        func=mybir.ActivationFunctionType.Identity,
                        bias=bias[:, t : t + 1],
                    )
                for t in range(HIDDEN_TILES):
                    nc.gpsimd.tensor_tensor(
                        out=agg_low[:].rearrange("p (a b t) -> p t a b", a=HALF, t=PACK)[:, t],
                        in0=parked[t][:].rearrange("p (a b) -> p a b", a=HALF),
                        in1=node_bias_for_all_types(t),
                        op=mybir.AluOpType.add,
                    )

        agg_rows = keep.tile([P, PACK * HALF_COLS], BF16, name="agg_rows")
        agg_high = keep.tile([P, PACK * HALF_COLS], BF16, name="agg_high", align_bytes=64)

        def high_passes(run):
            if is_last(run):
                second_product(agg_low, 0)
            edge_passes("high", run)
            if is_last(run):
                for t in range(HIDDEN_TILES):
                    nc.vector.tensor_tensor(
                        out=agg_rows[:, t * HALF_COLS : (t + 1) * HALF_COLS].rearrange("p (a b) -> p a b", a=HALF),
                        in0=acc["high"][t][:].rearrange("p (a b) -> p a b", a=HALF),
                        in1=node_bias_for_all_types(t),
                        op=mybir.AluOpType.add,
                    )
                nc.vector.tensor_copy(
                    out=agg_high[:].rearrange("p (c t) -> p c t", t=PACK),
                    in_=agg_rows[:].rearrange("p (t c) -> p c t", t=PACK),
                )
                second_product(agg_high, 1)

        def stream_run(name, n, passes):
            run = []
            blocks = []
            for g in range(n * RUN_BLOCKS, (n + 1) * RUN_BLOCKS):
                c, g_in_chunk = divmod(g, CHUNK_PASSES)
                codes, scales = new_codes()
                run.append((g, codes, scales))
                blocks.append(tiles_of_pass((name, c), g_in_chunk) + (codes[:], scales[:]))
            advance(blocks, later(passes, run))
            if (n + 1) * RUN_BLOCKS % CHUNK_PASSES == 0 and len(raws) < len(order):
                refill(1)

        for n in range(PASSES // LOW_RUN):
            run = []
            blocks = []
            for g in range(n * LOW_RUN, (n + 1) * LOW_RUN):
                c, g_in_chunk = divmod(g, CHUNK_PASSES)
                codes, scales = new_codes()
                run.append((g, codes, scales))
                cols = slice(g * HIDDEN, (g + 1) * HIDDEN)
                blocks.append(tiles_of_pass(("w_edge", c), g_in_chunk) + (w_edge_codes[:, cols], w_edge_scales[:, cols]))
                blocks.append(tiles_of_pass(("edge_low", c), g_in_chunk) + (codes[:], scales[:]))
            advance(blocks, later(low_passes, run))
            if (n + 1) * LOW_RUN % CHUNK_PASSES == 0:
                refill(2)

        image_words = raws["image", 0][:].bitcast(F32)
        for n in range(PASSES // (PACK * RUN_BLOCKS)):
            blocks = []
            for j in range(n * RUN_BLOCKS, (n + 1) * RUN_BLOCKS):
                cols = slice(j * BANK, (j + 1) * BANK)
                blocks.append((image_words, j * PACK * PASS_WORDS, PASS_WORDS, image_codes[:, cols], image_scales[:, cols]))
            advance(blocks, None)
        refill(1)

        for n in range(RUNS):
            stream_run("w_src", n, node_passes)

        for n in range(RUNS):
            m = n - RUNS // 2
            types_of_run = range(m * 2 * TYPES // RUNS, (m + 1) * 2 * TYPES // RUNS) if m >= 0 else range(0)
            fwd_grouped = {}
            for a in types_of_run:
                fwd_grouped[a] = small_pool.tile([P, PACK * REP], BF16, name="fwd_grouped", align_bytes=64)
                target = fwd_grouped[a][:].rearrange("p (r t) -> p r t", t=PACK)
                source = raws["fwd", 0][:, a * PACK * REP : (a + 1) * PACK * REP].rearrange("p (t r) -> p r t", t=PACK)
                if a % 2 == 0:
                    nc.scalar.copy(out=target, in_=source)
                else:
                    nc.vector.tensor_copy(out=target, in_=source)
            stream_run("edge_high", n, high_passes)
            for a in types_of_run:
                reps = slice(a * REP, (a + 1) * REP)
                quantise(fwd_grouped[a][:], fwd_codes[:, reps], fwd_scales[:, reps])

        advance([], None)
        advance([], None)
